import numpy as np
import ml_dtypes


def mxq(x, axis, fmt="e4m3"):
    dtype, down = {"e4m3": (ml_dtypes.float8_e4m3fn, 7), "e5m2": (ml_dtypes.float8_e5m2, 14)}[fmt]
    v = np.moveaxis(np.asarray(x, np.float32).astype(ml_dtypes.bfloat16).astype(np.float64), axis, -1)
    blocks = v.reshape(v.shape[:-1] + (-1, 32))
    amax = np.abs(blocks).max(-1, keepdims=True)
    byte = np.maximum(np.where(amax > 0, np.frexp(amax)[1] - 1 + 127, 0) - down, 1)
    scale = np.exp2(byte - 127.0)
    codes = (blocks / scale).astype(np.float32).astype(dtype).astype(np.float64)
    return np.moveaxis((codes * scale).reshape(v.shape), -1, axis)


WIDE = False


def mx_kscale(k):
    if not WIDE:
        return np.ones(k)
    levels = np.array([10, -10, 5, -5, 0])
    if k % 512:
        return np.exp2(np.random.permutation(np.resize(levels, k // 32))).repeat(32)
    a = np.empty((k // 512, 16))
    for p in range(k // 512):
        a[p, :8] = np.random.permutation(np.resize(levels, 8))
        for g in range(8):
            far = levels[np.abs(levels - a[p, g]) >= 10]
            a[p, g + 8] = far[np.random.randint(len(far))]
    return np.exp2(a.ravel()).repeat(32)


BF16 = ml_dtypes.bfloat16


def bf(x):
    return np.asarray(x, np.float32).astype(BF16)


def f64(x):
    return np.asarray(x).astype(np.float64)


N, V, EN1, EN2, D, K, EMB = 8192, 4096, 1024, 512, 128, 512, 1024
BN_EPS = 1e-5


def batchnorm(x):
    m = x.mean(axis=0)
    v = x.var(axis=0)
    return (x - m) * (1.0 / np.sqrt(v + BN_EPS))


def setup_inputs():
    s, t = mx_kscale(EN1), mx_kscale(EN2)
    return {
        "en1": bf(np.maximum(np.random.standard_normal((N, EN1)) * 1.15, 0.0) * s),
        "W2": bf(np.random.standard_normal((EN1, EN2)) / np.sqrt(EN1) / s[:, None] * t),
        "b2": bf(np.random.standard_normal(EN2) * 0.2 * t),
        "Wmean": bf(np.random.standard_normal((EN2, D)) / np.sqrt(EN2) / t[:, None]),
        "Wlogvar": bf(np.random.standard_normal((EN2, D)) / np.sqrt(EN2) / t[:, None]),
        "eps": bf(np.random.standard_normal((N, D))),
    }


def reference(en1, W2, b2, Wmean, Wlogvar, eps):
    en2 = np.maximum((mxq(f64(en1), 1, "e4m3") @ mxq(f64(W2), 0, "e4m3")) + f64(b2), 0.0)
    en2q = mxq(en2, 1, "e4m3")
    posterior_mean = batchnorm(en2q @ mxq(f64(Wmean), 0, "e4m3"))
    posterior_logvar = batchnorm(en2q @ mxq(f64(Wlogvar), 0, "e4m3"))
    posterior_var = np.exp(posterior_logvar)
    z = posterior_mean + np.sqrt(posterior_var) * f64(eps)
    zx = batchnorm(z)
    return z, zx

@@ -1,0 +1,400 @@
+from contextlib import ExitStack
+
+import concourse.mybir as mybir
+from concourse.masks import make_identity
+
+F32 = mybir.dt.float32
+BF16 = mybir.dt.bfloat16
+U32 = mybir.dt.uint32
+U8 = mybir.dt.uint8
+FP8X4 = mybir.dt.float8_e4m3fn_x4
+ACT = mybir.ActivationFunctionType
+ALU = mybir.AluOpType
+AXIS = mybir.AxisListType
+
+P = 128
+PACK = 4
+ROWS = 8192
+K1 = 1024
+K2 = 512
+D = 128
+PASSES1 = K1 // (P * PACK)
+BLOCK = 512
+NBLOCKS = ROWS // BLOCK
+SUB = BLOCK // P
+K2_TILES = K2 // P
+PSUM_BANKS = 8
+BN_EPS = 1e-5
+BN_STATS_DIM = 6
+LOADS_AHEAD = 3
+DRAIN_STEPS = 4
+M = 0
+LV = 1
+
+FLOPS = 2 * ROWS * (K1 * K2 + K2 * 2 * D)
+
+
+def block_cols(j):
+    return slice(j * BLOCK, (j + 1) * BLOCK)
+
+
+def block_rows(dram, j):
+    return dram[j * BLOCK : (j + 1) * BLOCK, :].rearrange("(r s) w -> r (s w)", s=SUB)
+
+
+def regrouped(grouped, planes):
+    return {
+        "out": grouped.rearrange("p (c i) t -> p c t i", i=4),
+        "in_": planes.rearrange("p t (c i) -> p c t i", i=4),
+    }
+
+
+def tile_modelvd_pa_t_kernel(tc, en1, W2, b2, Wmean, Wlogvar, eps, out_0, out_1):
+    nc = tc.nc
+    with ExitStack() as kernel_scope:
+        kernel_scope.enter_context(tc.manual_schedule())
+        keep = kernel_scope.enter_context(tc.tile_pool(name="keep", bufs=1))
+        psum = kernel_scope.enter_context(tc.psum_pool(name="psum", bufs=PSUM_BANKS))
+
+        ident_f32 = keep.tile([P, P], F32)
+        make_identity(nc, ident_f32[:])
+        ident_bf16 = keep.tile([P, P], BF16)
+        make_identity(nc, ident_bf16[:])
+        minus_half = keep.tile([P, 2], F32)
+        nc.gpsimd.memset(minus_half[:], -0.5)
+        one_four = keep.tile([P, 2], F32)
+        nc.gpsimd.memset(one_four[:, M : M + 1], 1.0)
+        nc.gpsimd.memset(one_four[:, LV : LV + 1], 4.0)
+
+        warm = keep.tile([P, 1], F32)
+        nc.vector.memset(warm[:], 0.0)
+        nc.scalar.activation(out=warm[:], in_=warm[:], func=ACT.Exp)
+
+        w2_codes = keep.tile([P, PASSES1, K2], U32, align_bytes=64)
+        w2_scales = keep.tile([P, PASSES1, K2], U8, align_bytes=64)
+        head_codes = keep.tile([P, 2, D], U32, align_bytes=64)
+        head_scales = keep.tile([P, 2, D], U8, align_bytes=64)
+        bias = keep.tile([P, K2_TILES], F32)
+        en2_codes = keep.tile([P, ROWS], U32, align_bytes=64)
+        en2_scales = keep.tile([P, ROWS], U8, align_bytes=64)
+        eps_t = keep.tile([P, ROWS], BF16)
+        stats = keep.tile([P, 2, NBLOCKS, BN_STATS_DIM], F32)
+
+        def head_product(i, j):
+            product = psum.tile([P, BLOCK], F32, tag="bank")
+            nc.tensor.matmul_mx(
+                out=product[:],
+                lhsT=head_codes[:, i, :].bitcast(FP8X4),
+                lhsT_scale=head_scales[:, i, :],
+                rhs=en2_codes[:, block_cols(j)].bitcast(FP8X4),
+                rhs_scale=en2_scales[:, block_cols(j)],
+                start=True,
+                stop=True,
+            )
+            return product
+
+        with ExitStack() as phase:
+            prep = phase.enter_context(tc.tile_pool(name="prep", bufs=1))
+            loads = phase.enter_context(tc.tile_pool(name="loads", bufs=LOADS_AHEAD + 1))
+            work = phase.enter_context(tc.tile_pool(name="work", bufs=2))
+
+            x_of = {}
+            grouped1_of = {}
+            en1_mx_of = {}
+            planes_of = {}
+            grouped2_of = {}
+            products_of = {}
+
+            def load_block(j):
+                x = loads.tile([P, SUB * K1], BF16, name="x")
+                nc.sync.dma_start(out=x[:], in_=block_rows(en1, j))
+                x_of[j] = x
+
+            def transpose_block(j):
+                words = x_of[j][:].bitcast(F32).rearrange("p (s w) -> p s w", s=SUB)
+                grouped1 = work.tile([P, PASSES1 * BLOCK * PACK], BF16, align_bytes=64)
+                pairs = grouped1[:].bitcast(F32).rearrange(
+                    "p (b s r u) -> p b s r u", b=2 * PASSES1, s=2, r=P, u=2
+                )
+                for b in range(2 * PASSES1):
+                    g, half = divmod(b, 2)
+                    xt = psum.tile([P, 2, 2, P], F32, tag="bank")
+                    for s in range(2):
+                        for u in range(2):
+                            first = 2 * g * P
+                            nc.tensor.transpose(
+                                xt[:, s, u, :],
+                                words[:, 2 * half + s, first + u : first + 2 * P : 2],
+                                ident_f32[:],
+                            )
+                    permuted = xt[:].rearrange("p s u r -> p s r u")
+                    if b == 2 and j % 2 == 0:
+                        nc.vector.tensor_copy(out=pairs[:, b], in_=permuted)
+                    else:
+                        nc.scalar.copy(out=pairs[:, b], in_=permuted)
+                grouped1_of[j] = grouped1
+
+            def quantise_en1(j):
+                codes = work.tile([P, PASSES1 * BLOCK], U32, name="en1_codes", align_bytes=64)
+                scales = work.tile([P, PASSES1 * BLOCK], U8, name="en1_scales", align_bytes=64)
+                nc.vector.quantize_mx(
+                    out=codes[:].bitcast(FP8X4), scales=scales[:], in_=grouped1_of[j][:]
+                )
+                en1_mx_of[j] = (codes, scales)
+
+            def first_product(j):
+                codes, scales = en1_mx_of[j]
+                planes = work.tile([P, K2_TILES, BLOCK], BF16)
+                for t in range(K2_TILES):
+                    h = psum.tile([P, BLOCK], F32, tag="bank")
+                    for g in range(PASSES1):
+                        nc.tensor.matmul_mx(
+                            out=h[:],
+                            lhsT=w2_codes[:, g, t * P : (t + 1) * P].bitcast(FP8X4),
+                            lhsT_scale=w2_scales[:, g, t * P : (t + 1) * P],
+                            rhs=codes[:, g * BLOCK : (g + 1) * BLOCK].bitcast(FP8X4),
+                            rhs_scale=scales[:, g * BLOCK : (g + 1) * BLOCK],
+                            start=(g == 0),
+                            stop=(g == PASSES1 - 1),
+                        )
+                    nc.scalar.activation(
+                        out=planes[:, t, :], in_=h[:], func=ACT.Relu, bias=bias[:, t : t + 1]
+                    )
+                planes_of[j] = planes
+
+            def regroup_en2(j):
+                grouped2 = work.tile([P, BLOCK, PACK], BF16, align_bytes=64)
+                nc.vector.tensor_copy(**regrouped(grouped2[:], planes_of[j][:]))
+                grouped2_of[j] = grouped2
+
+            def quantise_en2(j):
+                nc.vector.quantize_mx(
+                    out=en2_codes[:, block_cols(j)].bitcast(FP8X4),
+                    scales=en2_scales[:, block_cols(j)],
+                    in_=grouped2_of[j][:].rearrange("p c t -> p (c t)"),
+                )
+
+            def take_statistics(j):
+                for i in (M, LV):
+                    nc.vector.bn_stats(out=stats[:, i, j, :], in_=products_of[j][i][:])
+
+            def transpose_eps(first_block, blocks):
+                for j in range(first_block, first_block + blocks, 2):
+                    eps_ps = psum.tile([P, 2 * SUB, P], BF16, tag="bank")
+                    for c in range(2 * SUB):
+                        nc.tensor.transpose(
+                            eps_ps[:, c, :], eps_rows[:, j * SUB + c, :], ident_bf16[:]
+                        )
+                    nc.scalar.copy(
+                        out=eps_t[:, j * BLOCK : (j + 2) * BLOCK],
+                        in_=eps_ps[:].rearrange("p c r -> p (c r)"),
+                    )
+
+            def prepare_w2():
+                w2_grouped = prep.tile([P, PASSES1, K2, PACK], BF16, align_bytes=64)
+                for g, copy in ((0, nc.vector.tensor_copy), (1, nc.scalar.copy)):
+                    copy(
+                        out=w2_grouped[:, g].rearrange("p (t m) j -> p t m j", t=K2_TILES),
+                        in_=w2_rows[:, g].rearrange("p j (m t) -> p t m j", t=K2_TILES),
+                    )
+                for g in range(PASSES1):
+                    nc.vector.quantize_mx(
+                        out=w2_codes[:, g, :].bitcast(FP8X4),
+                        scales=w2_scales[:, g, :],
+                        in_=w2_grouped[:, g].rearrange("p c t -> p (c t)"),
+                    )
+
+            def prepare_bias_and_heads():
+                nc.vector.tensor_copy(out=bias[:], in_=b2_cols[:])
+                head_grouped = prep.tile([P, 2, D, PACK], BF16, align_bytes=64)
+                for i in (M, LV):
+                    nc.vector.tensor_copy(**regrouped(head_grouped[:, i], head_rows[:, i]))
+                nc.vector.quantize_mx(
+                    out=head_codes[:].rearrange("p i d -> p (i d)").bitcast(FP8X4),
+                    scales=head_scales[:].rearrange("p i d -> p (i d)"),
+                    in_=head_grouped[:].rearrange("p i d t -> p (i d t)"),
+                )
+
+            w2_rows = prep.tile([P, PASSES1, PACK, K2], BF16)
+            nc.sync.dma_start(
+                out=w2_rows[:].rearrange("p g j c -> p g (j c)"),
+                in_=W2.rearrange("(g p j) c -> p g (j c)", p=P, j=PACK),
+            )
+            load_block(0)
+            b2_cols = prep.tile([P, K2_TILES], BF16)
+            nc.sync.dma_start(out=b2_cols[:], in_=b2.rearrange("(p t) -> p t", t=K2_TILES))
+            head_rows = prep.tile([P, 2, PACK, D], BF16)
+            for i, weight in ((M, Wmean), (LV, Wlogvar)):
+                nc.sync.dma_start(
+                    out=head_rows[:, i], in_=weight.rearrange("(p t) d -> p t d", t=PACK)
+                )
+            load_block(1)
+            load_block(2)
+            eps_rows = prep.tile([P, NBLOCKS * SUB, D], BF16)
+
+            prepare_w2()
+            transpose_block(0)
+            quantise_en1(0)
+            prepare_bias_and_heads()
+            for i in range(NBLOCKS + 3):
+                if i >= 3:
+                    take_statistics(i - 3)
+                if i + LOADS_AHEAD < NBLOCKS:
+                    load_block(i + LOADS_AHEAD)
+                if i + LOADS_AHEAD == NBLOCKS:
+                    nc.sync.dma_start(
+                        out=eps_rows[:].rearrange("r (j s) d -> r j (s d)", s=SUB),
+                        in_=eps.rearrange("(j r s) d -> r j (s d)", r=P, s=SUB),
+                    )
+                if i + 1 < NBLOCKS:
+                    transpose_block(i + 1)
+                if 1 <= i <= NBLOCKS:
+                    regroup_en2(i - 1)
+                if i + 1 < NBLOCKS:
+                    quantise_en1(i + 1)
+                if 1 <= i <= NBLOCKS:
+                    quantise_en2(i - 1)
+                if i < NBLOCKS:
+                    first_product(i)
+                if 2 <= i <= NBLOCKS + 1:
+                    products_of[i - 2] = (head_product(M, i - 2), head_product(LV, i - 2))
+                if i >= NBLOCKS + 3 - DRAIN_STEPS:
+                    share = NBLOCKS // DRAIN_STEPS
+                    transpose_eps((i - (NBLOCKS + 3 - DRAIN_STEPS)) * share, share)
+
+        with ExitStack() as phase:
+            small = phase.enter_context(tc.tile_pool(name="small", bufs=1))
+            tail = phase.enter_context(tc.tile_pool(name="tail", bufs=4))
+            staging = phase.enter_context(tc.tile_pool(name="staging", bufs=6))
+
+            lv_of = {0: head_product(LV, 0)}
+            m_of = {}
+            std_of = {}
+            noise_of = {}
+
+            mean_var = small.tile([P, 2, 2], F32)
+            for i in (LV, M):
+                nc.vector.bn_aggr(
+                    out=mean_var[:, i, :], in_=stats[:, i].rearrange("p j v -> p (j v)")
+                )
+            padded = small.tile([P, 2], F32)
+            nc.vector.scalar_tensor_tensor(
+                out=padded[:], in0=mean_var[:, :, 1], scalar=BN_EPS, in1=one_four[:],
+                op0=ALU.add, op1=ALU.mult,
+            )
+            factor = small.tile([P, 2], F32)
+            nc.gpsimd.tensor_tensor(out=factor[:], in0=padded[:], in1=minus_half[:], op=ALU.pow)
+            shift = small.tile([P, 2], F32)
+            nc.vector.scalar_tensor_tensor(
+                out=shift[:], in0=mean_var[:, :, 0], scalar=-1.0, in1=factor[:],
+                op0=ALU.mult, op1=ALU.mult,
+            )
+            shift_ps = psum.tile([P, D], F32, tag="bank")
+            nc.tensor.matmul(
+                out=shift_ps[:], lhsT=shift[:, M : M + 1].to_broadcast([P, P]), rhs=ident_f32[:],
+                start=True, stop=True,
+            )
+            shift_row = small.tile([P, D], F32)
+            nc.vector.tensor_copy(out=shift_row[:], in_=shift_ps[:])
+
+            z_less_shift = small.tile([P, ROWS], F32)
+            z_sums = small.tile([P, 2, NBLOCKS], F32)
+
+            def std_block(j):
+                std = tail.tile([P, BLOCK], F32)
+                nc.scalar.activation(
+                    out=std[:], in_=lv_of[j][:], func=ACT.Exp,
+                    bias=shift[:, LV : LV + 1], scale=factor[:, LV : LV + 1],
+                )
+                std_of[j] = std
+
+            def noise_block(j):
+                noise = tail.tile([P, BLOCK], F32)
+                nc.gpsimd.tensor_tensor(
+                    out=noise[:], in0=std_of[j][:], in1=eps_t[:, block_cols(j)], op=ALU.mult
+                )
+                noise_of[j] = noise
+
+            def sample_block(j):
+                nc.vector.scalar_tensor_tensor(
+                    out=z_less_shift[:, block_cols(j)], in0=m_of[j][:],
+                    scalar=factor[:, M : M + 1], in1=noise_of[j][:],
+                    op0=ALU.mult, op1=ALU.add, accum_out=z_sums[:, 0, j : j + 1],
+                )
+
+            def square_block(j):
+                squares = tail.tile([P, BLOCK], F32)
+                nc.scalar.activation(
+                    out=squares[:], in_=z_less_shift[:, block_cols(j)], func=ACT.Square,
+                    bias=shift[:, M : M + 1], accum_out=z_sums[:, 1, j : j + 1],
+                )
+
+            def transpose_back(source):
+                back = psum.tile([P, SUB, D], F32, tag="bank")
+                for s in range(SUB):
+                    nc.tensor.transpose(back[:, s, :], source[:, s * P : (s + 1) * P], ident_f32[:])
+                return back
+
+            def store_z(j):
+                back = transpose_back(z_less_shift[:, block_cols(j)])
+                z_rows = staging.tile([P, SUB, D], F32)
+                nc.vector.tensor_tensor(
+                    out=z_rows[:], in0=back[:],
+                    in1=shift_row[:].unsqueeze(1).to_broadcast([P, SUB, D]), op=ALU.add,
+                )
+                nc.sync.dma_start(
+                    out=block_rows(out_0, j), in_=z_rows[:].rearrange("r s d -> r (s d)")
+                )
+
+            for j in range(NBLOCKS + 4):
+                if j + 1 < NBLOCKS:
+                    lv_of[j + 1] = head_product(LV, j + 1)
+                if 1 <= j <= NBLOCKS:
+                    m_of[j - 1] = head_product(M, j - 1)
+                if j < NBLOCKS:
+                    std_block(j)
+                if 1 <= j <= NBLOCKS:
+                    noise_block(j - 1)
+                if 2 <= j <= NBLOCKS + 1:
+                    sample_block(j - 2)
+                if j >= 4:
+                    square_block(j - 4)
+                    store_z(j - 4)
+
+            z_sum = small.tile([P, 2], F32)
+            nc.vector.tensor_reduce(out=z_sum[:], in_=z_sums[:], axis=AXIS.X, op=ALU.add)
+            z_mean = small.tile([P, 1], F32)
+            nc.vector.tensor_scalar(
+                out=z_mean[:], in0=z_sum[:, 0:1], scalar1=1.0 / ROWS, scalar2=shift[:, M : M + 1],
+                op0=ALU.mult, op1=ALU.add,
+            )
+            z_mean2_less_eps = small.tile([P, 1], F32)
+            nc.vector.tensor_scalar(
+                out=z_mean2_less_eps[:], in0=z_mean[:], scalar1=z_mean[:], scalar2=BN_EPS,
+                op0=ALU.mult, op1=ALU.subtract,
+            )
+            z_padded = small.tile([P, 1], F32)
+            nc.vector.tensor_scalar(
+                out=z_padded[:], in0=z_sum[:, 1:2], scalar1=1.0 / ROWS,
+                scalar2=z_mean2_less_eps[:], op0=ALU.mult, op1=ALU.subtract,
+            )
+            z_factor = small.tile([P, 1], F32)
+            nc.gpsimd.tensor_tensor(
+                out=z_factor[:], in0=z_padded[:], in1=minus_half[:, 0:1], op=ALU.pow
+            )
+            zx_shift = small.tile([P, 1], F32)
+            nc.vector.tensor_scalar(
+                out=zx_shift[:], in0=z_sum[:, 0:1], scalar1=-1.0 / ROWS, scalar2=z_factor[:],
+                op0=ALU.mult, op1=ALU.mult,
+            )
+
+            for j in range(NBLOCKS):
+                zx_t = tail.tile([P, BLOCK], F32)
+                nc.vector.tensor_scalar(
+                    out=zx_t[:], in0=z_less_shift[:, block_cols(j)], scalar1=z_factor[:],
+                    scalar2=zx_shift[:], op0=ALU.mult, op1=ALU.add,
+                )
+                back = transpose_back(zx_t[:])
+                zx_rows = staging.tile([P, SUB * D], F32)
+                nc.scalar.copy(out=zx_rows[:], in_=back[:].rearrange("r s d -> r (s d)"))
+                nc.sync.dma_start(out=block_rows(out_1, j), in_=zx_rows[:])

@@ -30,6 +30,7 @@ LOADS_AHEAD = 3
 DRAIN_STEPS = 4
 M = 0
 LV = 1
+SORTED = 2
 
 FLOPS = 2 * ROWS * (K1 * K2 + K2 * 2 * D)
 
@@ -99,6 +100,7 @@ def tile_modelvd_pa_t_kernel(tc, en1, W2, b2, Wmean, Wlogvar, eps, out_0, out_1)
             work = phase.enter_context(tc.tile_pool(name="work", bufs=2))
 
             x_of = {}
+            sorted_of = {}
             grouped1_of = {}
             en1_mx_of = {}
             planes_of = {}
@@ -110,6 +112,12 @@ def tile_modelvd_pa_t_kernel(tc, en1, W2, b2, Wmean, Wlogvar, eps, out_0, out_1)
                 nc.sync.dma_start(out=x[:], in_=block_rows(en1, j))
                 x_of[j] = x
 
+            def sort_words(j):
+                words = x_of[j][:].bitcast(F32).rearrange("p (s w u) -> p s u w", s=SUB, u=2)
+                in_order = work.tile([P, SORTED, 2, K1 // 4], F32)
+                nc.vector.tensor_copy(out=in_order[:], in_=words[:, 0:SORTED])
+                sorted_of[j] = in_order
+
             def transpose_block(j):
                 words = x_of[j][:].bitcast(F32).rearrange("p (s w) -> p s w", s=SUB)
                 grouped1 = work.tile([P, PASSES1 * BLOCK * PACK], BF16, align_bytes=64)
@@ -120,18 +128,14 @@ def tile_modelvd_pa_t_kernel(tc, en1, W2, b2, Wmean, Wlogvar, eps, out_0, out_1)
                     g, half = divmod(b, 2)
                     xt = psum.tile([P, 2, 2, P], F32, tag="bank")
                     for s in range(2):
+                        piece = 2 * half + s
                         for u in range(2):
-                            first = 2 * g * P
-                            nc.tensor.transpose(
-                                xt[:, s, u, :],
-                                words[:, 2 * half + s, first + u : first + 2 * P : 2],
-                                ident_f32[:],
-                            )
-                    permuted = xt[:].rearrange("p s u r -> p s r u")
-                    if b == 2 and j % 2 == 0:
-                        nc.vector.tensor_copy(out=pairs[:, b], in_=permuted)
-                    else:
-                        nc.scalar.copy(out=pairs[:, b], in_=permuted)
+                            if piece < SORTED:
+                                taken = sorted_of[j][:, piece, u, g * P : (g + 1) * P]
+                            else:
+                                taken = words[:, piece, 2 * g * P + u : 2 * (g + 1) * P : 2]
+                            nc.tensor.transpose(xt[:, s, u, :], taken, ident_f32[:])
+                    nc.scalar.copy(out=pairs[:, b], in_=xt[:].rearrange("p s u r -> p s r u"))
                 grouped1_of[j] = grouped1
 
             def quantise_en1(j):
@@ -233,6 +237,8 @@ def tile_modelvd_pa_t_kernel(tc, en1, W2, b2, Wmean, Wlogvar, eps, out_0, out_1)
             eps_rows = prep.tile([P, NBLOCKS * SUB, D], BF16)
 
             prepare_w2()
+            sort_words(0)
+            sort_words(1)
             transpose_block(0)
             quantise_en1(0)
             prepare_bias_and_heads()
@@ -246,6 +252,8 @@ def tile_modelvd_pa_t_kernel(tc, en1, W2, b2, Wmean, Wlogvar, eps, out_0, out_1)
                         out=eps_rows[:].rearrange("r (j s) d -> r j (s d)", s=SUB),
                         in_=eps.rearrange("(j r s) d -> r j (s d)", r=P, s=SUB),
                     )
+                if i + 2 < NBLOCKS:
+                    sort_words(i + 2)
                 if i + 1 < NBLOCKS:
                     transpose_block(i + 1)
                 if 1 <= i <= NBLOCKS:

@@ -27,9 +27,9 @@ PSUM_BANKS = 8
 BN_EPS = 1e-5
 BN_STATS_DIM = 6
 LOADS_AHEAD = 3
-DRAIN_STEPS = 4
 M = 0
 LV = 1
+HALF = BLOCK // 2
 SORTED = 2
 
 FLOPS = 2 * ROWS * (K1 * K2 + K2 * 2 * D)
@@ -61,11 +61,8 @@ def tile_modelvd_pa_t_kernel(tc, en1, W2, b2, Wmean, Wlogvar, eps, out_0, out_1)
         make_identity(nc, ident_f32[:])
         ident_bf16 = keep.tile([P, P], BF16)
         make_identity(nc, ident_bf16[:])
-        minus_half = keep.tile([P, 2], F32)
+        minus_half = keep.tile([P, 1], F32)
         nc.gpsimd.memset(minus_half[:], -0.5)
-        one_four = keep.tile([P, 2], F32)
-        nc.gpsimd.memset(one_four[:, M : M + 1], 1.0)
-        nc.gpsimd.memset(one_four[:, LV : LV + 1], 4.0)
 
         warm = keep.tile([P, 1], F32)
         nc.vector.memset(warm[:], 0.0)
@@ -78,8 +75,15 @@ def tile_modelvd_pa_t_kernel(tc, en1, W2, b2, Wmean, Wlogvar, eps, out_0, out_1)
         bias = keep.tile([P, K2_TILES], F32)
         en2_codes = keep.tile([P, ROWS], U32, align_bytes=64)
         en2_scales = keep.tile([P, ROWS], U8, align_bytes=64)
+        eps_rows = keep.tile([P, NBLOCKS * SUB, D], BF16)
         eps_t = keep.tile([P, ROWS], BF16)
         stats = keep.tile([P, 2, NBLOCKS, BN_STATS_DIM], F32)
+        mean_var = keep.tile([P, 2, 2], F32)
+        padded = keep.tile([P, 2], F32)
+        factor = keep.tile([P, 2], F32)
+        shift = keep.tile([P, 2], F32)
+        shift_row = keep.tile([P, D], F32)
+        z_sums = keep.tile([P, 2, NBLOCKS + 1], F32)
 
         def head_product(i, j):
             product = psum.tile([P, BLOCK], F32, tag="bank")
@@ -107,9 +111,12 @@ def tile_modelvd_pa_t_kernel(tc, en1, W2, b2, Wmean, Wlogvar, eps, out_0, out_1)
             grouped2_of = {}
             products_of = {}
 
-            def load_block(j):
+            def load_block(j, pieces=1):
                 x = loads.tile([P, SUB * K1], BF16, name="x")
-                nc.sync.dma_start(out=x[:], in_=block_rows(en1, j))
+                width = SUB * K1 // pieces
+                for c in range(pieces):
+                    cols = slice(c * width, (c + 1) * width)
+                    nc.sync.dma_start(out=x[:, cols], in_=block_rows(en1, j)[:, cols])
                 x_of[j] = x
 
             def sort_words(j):
@@ -122,65 +129,89 @@ def tile_modelvd_pa_t_kernel(tc, en1, W2, b2, Wmean, Wlogvar, eps, out_0, out_1)
                 words = x_of[j][:].bitcast(F32).rearrange("p (s w) -> p s w", s=SUB)
                 grouped1 = work.tile([P, PASSES1 * BLOCK * PACK], BF16, align_bytes=64)
                 pairs = grouped1[:].bitcast(F32).rearrange(
-                    "p (b s r u) -> p b s r u", b=2 * PASSES1, s=2, r=P, u=2
+                    "p (g h s r u) -> p g h s r u", g=PASSES1, h=2, s=2, r=P, u=2
                 )
-                for b in range(2 * PASSES1):
-                    g, half = divmod(b, 2)
-                    xt = psum.tile([P, 2, 2, P], F32, tag="bank")
-                    for s in range(2):
-                        piece = 2 * half + s
-                        for u in range(2):
-                            if piece < SORTED:
-                                taken = sorted_of[j][:, piece, u, g * P : (g + 1) * P]
-                            else:
-                                taken = words[:, piece, 2 * g * P + u : 2 * (g + 1) * P : 2]
-                            nc.tensor.transpose(xt[:, s, u, :], taken, ident_f32[:])
-                    nc.scalar.copy(out=pairs[:, b], in_=xt[:].rearrange("p s u r -> p s r u"))
+                for half in range(2):
+                    for g in range(PASSES1):
+                        xt = psum.tile([P, 2, 2, P], F32, tag="bank")
+                        for s in range(2):
+                            piece = 2 * half + s
+                            for u in range(2):
+                                if j in sorted_of and piece < SORTED:
+                                    taken = sorted_of[j][:, piece, u, g * P : (g + 1) * P]
+                                else:
+                                    taken = words[:, piece, 2 * g * P + u : 2 * (g + 1) * P : 2]
+                                nc.tensor.transpose(xt[:, s, u, :], taken, ident_f32[:])
+                        nc.scalar.copy(
+                            out=pairs[:, g, half], in_=xt[:].rearrange("p s u r -> p s r u")
+                        )
                 grouped1_of[j] = grouped1
 
-            def quantise_en1(j):
+            def quantise_en1(j, pieces=1):
                 codes = work.tile([P, PASSES1 * BLOCK], U32, name="en1_codes", align_bytes=64)
                 scales = work.tile([P, PASSES1 * BLOCK], U8, name="en1_scales", align_bytes=64)
-                nc.vector.quantize_mx(
-                    out=codes[:].bitcast(FP8X4), scales=scales[:], in_=grouped1_of[j][:]
-                )
+                if pieces == 1:
+                    runs = [slice(0, PASSES1 * BLOCK)]
+                else:
+                    runs = [
+                        slice(g * BLOCK + half * HALF, g * BLOCK + (half + 1) * HALF)
+                        for half in range(2)
+                        for g in range(PASSES1)
+                    ]
+                for run in runs:
+                    nc.vector.quantize_mx(
+                        out=codes[:, run].bitcast(FP8X4),
+                        scales=scales[:, run],
+                        in_=grouped1_of[j][:, run.start * PACK : run.stop * PACK],
+                    )
                 en1_mx_of[j] = (codes, scales)
 
-            def first_product(j):
+            def first_product(j, pieces=1):
                 codes, scales = en1_mx_of[j]
                 planes = work.tile([P, K2_TILES, BLOCK], BF16)
-                for t in range(K2_TILES):
-                    h = psum.tile([P, BLOCK], F32, tag="bank")
-                    for g in range(PASSES1):
-                        nc.tensor.matmul_mx(
-                            out=h[:],
-                            lhsT=w2_codes[:, g, t * P : (t + 1) * P].bitcast(FP8X4),
-                            lhsT_scale=w2_scales[:, g, t * P : (t + 1) * P],
-                            rhs=codes[:, g * BLOCK : (g + 1) * BLOCK].bitcast(FP8X4),
-                            rhs_scale=scales[:, g * BLOCK : (g + 1) * BLOCK],
-                            start=(g == 0),
-                            stop=(g == PASSES1 - 1),
+                width = BLOCK // pieces
+                for c in range(pieces):
+                    for t in range(K2_TILES):
+                        h = psum.tile([P, width], F32, tag="bank")
+                        for g in range(PASSES1):
+                            run = slice(g * BLOCK + c * width, g * BLOCK + (c + 1) * width)
+                            nc.tensor.matmul_mx(
+                                out=h[:],
+                                lhsT=w2_codes[:, g, t * P : (t + 1) * P].bitcast(FP8X4),
+                                lhsT_scale=w2_scales[:, g, t * P : (t + 1) * P],
+                                rhs=codes[:, run].bitcast(FP8X4),
+                                rhs_scale=scales[:, run],
+                                start=(g == 0),
+                                stop=(g == PASSES1 - 1),
+                            )
+                        nc.scalar.activation(
+                            out=planes[:, t, c * width : (c + 1) * width], in_=h[:],
+                            func=ACT.Relu, bias=bias[:, t : t + 1],
                         )
-                    nc.scalar.activation(
-                        out=planes[:, t, :], in_=h[:], func=ACT.Relu, bias=bias[:, t : t + 1]
-                    )
                 planes_of[j] = planes
 
-            def regroup_en2(j):
+            def regroup_en2(j, engines=(nc.vector.tensor_copy,)):
                 grouped2 = work.tile([P, BLOCK, PACK], BF16, align_bytes=64)
-                nc.vector.tensor_copy(**regrouped(grouped2[:], planes_of[j][:]))
+                width = BLOCK // len(engines)
+                for c, copy in enumerate(engines):
+                    cols = slice(c * width, (c + 1) * width)
+                    copy(**regrouped(grouped2[:, cols], planes_of[j][:, :, cols]))
                 grouped2_of[j] = grouped2
 
-            def quantise_en2(j):
-                nc.vector.quantize_mx(
-                    out=en2_codes[:, block_cols(j)].bitcast(FP8X4),
-                    scales=en2_scales[:, block_cols(j)],
-                    in_=grouped2_of[j][:].rearrange("p c t -> p (c t)"),
-                )
+            def quantise_en2(j, pieces=1):
+                width = BLOCK // pieces
+                for c in range(pieces):
+                    cols = slice(j * BLOCK + c * width, j * BLOCK + (c + 1) * width)
+                    nc.vector.quantize_mx(
+                        out=en2_codes[:, cols].bitcast(FP8X4),
+                        scales=en2_scales[:, cols],
+                        in_=grouped2_of[j][:, c * width : (c + 1) * width].rearrange(
+                            "p c t -> p (c t)"
+                        ),
+                    )
 
-            def take_statistics(j):
-                for i in (M, LV):
-                    nc.vector.bn_stats(out=stats[:, i, j, :], in_=products_of[j][i][:])
+            def take_statistics(i, j):
+                nc.vector.bn_stats(out=stats[:, i, j, :], in_=products_of[j][i][:])
 
             def transpose_eps(first_block, blocks):
                 for j in range(first_block, first_block + blocks, 2):
@@ -196,11 +227,17 @@ def tile_modelvd_pa_t_kernel(tc, en1, W2, b2, Wmean, Wlogvar, eps, out_0, out_1)
 
             def prepare_w2():
                 w2_grouped = prep.tile([P, PASSES1, K2, PACK], BF16, align_bytes=64)
-                for g, copy in ((0, nc.vector.tensor_copy), (1, nc.scalar.copy)):
+
+                def regroup_w2(copy, g, first_tile, last_tile):
+                    tiles = slice(first_tile, last_tile)
                     copy(
-                        out=w2_grouped[:, g].rearrange("p (t m) j -> p t m j", t=K2_TILES),
-                        in_=w2_rows[:, g].rearrange("p j (m t) -> p t m j", t=K2_TILES),
+                        out=w2_grouped[:, g].rearrange("p (t m) j -> p t m j", t=K2_TILES)[:, tiles],
+                        in_=w2_rows[:, g].rearrange("p j (m t) -> p t m j", t=K2_TILES)[:, tiles],
                     )
+
+                regroup_w2(nc.vector.tensor_copy, 0, 0, K2_TILES)
+                regroup_w2(nc.scalar.copy, 1, K2_TILES // 2, K2_TILES)
+                regroup_w2(nc.vector.tensor_copy, 1, 0, K2_TILES // 2)
                 for g in range(PASSES1):
                     nc.vector.quantize_mx(
                         out=w2_codes[:, g, :].bitcast(FP8X4),
@@ -208,8 +245,7 @@ def tile_modelvd_pa_t_kernel(tc, en1, W2, b2, Wmean, Wlogvar, eps, out_0, out_1)
                         in_=w2_grouped[:, g].rearrange("p c t -> p (c t)"),
                     )
 
-            def prepare_bias_and_heads():
-                nc.vector.tensor_copy(out=bias[:], in_=b2_cols[:])
+            def prepare_heads():
                 head_grouped = prep.tile([P, 2, D, PACK], BF16, align_bytes=64)
                 for i in (M, LV):
                     nc.vector.tensor_copy(**regrouped(head_grouped[:, i], head_rows[:, i]))
@@ -220,31 +256,35 @@ def tile_modelvd_pa_t_kernel(tc, en1, W2, b2, Wmean, Wlogvar, eps, out_0, out_1)
                 )
 
             w2_rows = prep.tile([P, PASSES1, PACK, K2], BF16)
-            nc.sync.dma_start(
-                out=w2_rows[:].rearrange("p g j c -> p g (j c)"),
-                in_=W2.rearrange("(g p j) c -> p g (j c)", p=P, j=PACK),
-            )
-            load_block(0)
+            for g in range(PASSES1):
+                nc.sync.dma_start(
+                    out=w2_rows[:, g].rearrange("p j c -> p (j c)"),
+                    in_=W2[g * P * PACK : (g + 1) * P * PACK, :].rearrange(
+                        "(p j) c -> p (j c)", j=PACK
+                    ),
+                )
+            load_block(0, pieces=2)
             b2_cols = prep.tile([P, K2_TILES], BF16)
             nc.sync.dma_start(out=b2_cols[:], in_=b2.rearrange("(p t) -> p t", t=K2_TILES))
+            load_block(1)
             head_rows = prep.tile([P, 2, PACK, D], BF16)
             for i, weight in ((M, Wmean), (LV, Wlogvar)):
                 nc.sync.dma_start(
                     out=head_rows[:, i], in_=weight.rearrange("(p t) d -> p t d", t=PACK)
                 )
-            load_block(1)
             load_block(2)
-            eps_rows = prep.tile([P, NBLOCKS * SUB, D], BF16)
 
             prepare_w2()
-            sort_words(0)
-            sort_words(1)
             transpose_block(0)
-            quantise_en1(0)
-            prepare_bias_and_heads()
-            for i in range(NBLOCKS + 3):
-                if i >= 3:
-                    take_statistics(i - 3)
+            quantise_en1(0, pieces=2)
+            nc.gpsimd.tensor_copy(out=bias[:], in_=b2_cols[:])
+            first_product(0, pieces=2)
+            transpose_block(1)
+            prepare_heads()
+            quantise_en1(1)
+            load_block(LOADS_AHEAD)
+
+            for i in range(1, NBLOCKS - 1):
                 if i + LOADS_AHEAD < NBLOCKS:
                     load_block(i + LOADS_AHEAD)
                 if i + LOADS_AHEAD == NBLOCKS:
@@ -252,61 +292,85 @@ def tile_modelvd_pa_t_kernel(tc, en1, W2, b2, Wmean, Wlogvar, eps, out_0, out_1)
                         out=eps_rows[:].rearrange("r (j s) d -> r j (s d)", s=SUB),
                         in_=eps.rearrange("(j r s) d -> r j (s d)", r=P, s=SUB),
                     )
+                if i >= 2:
+                    for head in (M, LV):
+                        take_statistics(head, i - 2)
+                regroup_en2(i - 1)
                 if i + 2 < NBLOCKS:
                     sort_words(i + 2)
-                if i + 1 < NBLOCKS:
-                    transpose_block(i + 1)
-                if 1 <= i <= NBLOCKS:
-                    regroup_en2(i - 1)
-                if i + 1 < NBLOCKS:
-                    quantise_en1(i + 1)
-                if 1 <= i <= NBLOCKS:
-                    quantise_en2(i - 1)
-                if i < NBLOCKS:
-                    first_product(i)
-                if 2 <= i <= NBLOCKS + 1:
-                    products_of[i - 2] = (head_product(M, i - 2), head_product(LV, i - 2))
-                if i >= NBLOCKS + 3 - DRAIN_STEPS:
-                    share = NBLOCKS // DRAIN_STEPS
-                    transpose_eps((i - (NBLOCKS + 3 - DRAIN_STEPS)) * share, share)
+                transpose_block(i + 1)
+                quantise_en2(i - 1)
+                quantise_en1(i + 1)
+                first_product(i)
+                products_of[i - 1] = {head: head_product(head, i - 1) for head in (M, LV)}
+
+            last = NBLOCKS - 1
+            for head in (M, LV):
+                take_statistics(head, last - 2)
+            regroup_en2(last - 1)
+            first_product(last, pieces=2)
+            transpose_eps(0, 4)
+            quantise_en2(last - 1)
+            regroup_en2(last, engines=(nc.vector.tensor_copy, nc.scalar.copy))
+            products_of[last - 1] = {head: head_product(head, last - 1) for head in (LV, M)}
+            quantise_en2(last, pieces=2)
+            products_of[last] = {head: head_product(head, last) for head in (LV, M)}
+            transpose_eps(4, NBLOCKS - 4)
 
         with ExitStack() as phase:
             small = phase.enter_context(tc.tile_pool(name="small", bufs=1))
             tail = phase.enter_context(tc.tile_pool(name="tail", bufs=4))
             staging = phase.enter_context(tc.tile_pool(name="staging", bufs=6))
 
+            def finish_statistics(i):
+                nc.vector.bn_aggr(
+                    out=mean_var[:, i, :], in_=stats[:, i].rearrange("p j v -> p (j v)")
+                )
+                nc.vector.tensor_scalar(
+                    out=padded[:, i : i + 1], in0=mean_var[:, i, 1:2], scalar1=BN_EPS,
+                    scalar2=4.0 if i == LV else 1.0, op0=ALU.add, op1=ALU.mult,
+                )
+                nc.gpsimd.tensor_tensor(
+                    out=factor[:, i : i + 1], in0=padded[:, i : i + 1], in1=minus_half[:],
+                    op=ALU.pow,
+                )
+
+            def make_shift(i):
+                nc.vector.scalar_tensor_tensor(
+                    out=shift[:, i : i + 1], in0=mean_var[:, i, 0:1], scalar=-1.0,
+                    in1=factor[:, i : i + 1], op0=ALU.mult, op1=ALU.mult,
+                )
+
+            for j in (last - 1, last):
+                take_statistics(LV, j)
+            finish_statistics(LV)
+            for j in (last - 1, last):
+                take_statistics(M, j)
+            finish_statistics(M)
+            make_shift(LV)
+            make_shift(M)
+            nc.vector.tensor_scalar(
+                out=z_sums[:, 0, NBLOCKS:], in0=shift[:, M : M + 1], scalar1=float(ROWS),
+                scalar2=None, op0=ALU.mult,
+            )
+            nc.vector.tensor_scalar(
+                out=z_sums[:, 1, NBLOCKS:], in0=minus_half[:], scalar1=0.0,
+                scalar2=ROWS * BN_EPS, op0=ALU.mult, op1=ALU.add,
+            )
+
             lv_of = {0: head_product(LV, 0)}
             m_of = {}
             std_of = {}
             noise_of = {}
 
-            mean_var = small.tile([P, 2, 2], F32)
-            for i in (LV, M):
-                nc.vector.bn_aggr(
-                    out=mean_var[:, i, :], in_=stats[:, i].rearrange("p j v -> p (j v)")
-                )
-            padded = small.tile([P, 2], F32)
-            nc.vector.scalar_tensor_tensor(
-                out=padded[:], in0=mean_var[:, :, 1], scalar=BN_EPS, in1=one_four[:],
-                op0=ALU.add, op1=ALU.mult,
-            )
-            factor = small.tile([P, 2], F32)
-            nc.gpsimd.tensor_tensor(out=factor[:], in0=padded[:], in1=minus_half[:], op=ALU.pow)
-            shift = small.tile([P, 2], F32)
-            nc.vector.scalar_tensor_tensor(
-                out=shift[:], in0=mean_var[:, :, 0], scalar=-1.0, in1=factor[:],
-                op0=ALU.mult, op1=ALU.mult,
-            )
             shift_ps = psum.tile([P, D], F32, tag="bank")
             nc.tensor.matmul(
                 out=shift_ps[:], lhsT=shift[:, M : M + 1].to_broadcast([P, P]), rhs=ident_f32[:],
                 start=True, stop=True,
             )
-            shift_row = small.tile([P, D], F32)
             nc.vector.tensor_copy(out=shift_row[:], in_=shift_ps[:])
 
             z_less_shift = small.tile([P, ROWS], F32)
-            z_sums = small.tile([P, 2, NBLOCKS], F32)
 
             def std_block(j):
                 std = tail.tile([P, BLOCK], F32)
@@ -354,7 +418,7 @@ def tile_modelvd_pa_t_kernel(tc, en1, W2, b2, Wmean, Wlogvar, eps, out_0, out_1)
                     out=block_rows(out_0, j), in_=z_rows[:].rearrange("r s d -> r (s d)")
                 )
 
-            for j in range(NBLOCKS + 4):
+            for j in range(NBLOCKS + 2):
                 if j + 1 < NBLOCKS:
                     lv_of[j + 1] = head_product(LV, j + 1)
                 if 1 <= j <= NBLOCKS:
@@ -363,46 +427,49 @@ def tile_modelvd_pa_t_kernel(tc, en1, W2, b2, Wmean, Wlogvar, eps, out_0, out_1)
                     std_block(j)
                 if 1 <= j <= NBLOCKS:
                     noise_block(j - 1)
-                if 2 <= j <= NBLOCKS + 1:
+                if 2 <= j:
                     sample_block(j - 2)
+                if j >= 3:
+                    square_block(j - 3)
                 if j >= 4:
-                    square_block(j - 4)
                     store_z(j - 4)
+            square_block(last)
+            store_z(last - 1)
 
             z_sum = small.tile([P, 2], F32)
             nc.vector.tensor_reduce(out=z_sum[:], in_=z_sums[:], axis=AXIS.X, op=ALU.add)
-            z_mean = small.tile([P, 1], F32)
-            nc.vector.tensor_scalar(
-                out=z_mean[:], in0=z_sum[:, 0:1], scalar1=1.0 / ROWS, scalar2=shift[:, M : M + 1],
-                op0=ALU.mult, op1=ALU.add,
-            )
-            z_mean2_less_eps = small.tile([P, 1], F32)
-            nc.vector.tensor_scalar(
-                out=z_mean2_less_eps[:], in0=z_mean[:], scalar1=z_mean[:], scalar2=BN_EPS,
-                op0=ALU.mult, op1=ALU.subtract,
+            z_mean2 = small.tile([P, 1], F32)
+            nc.vector.scalar_tensor_tensor(
+                out=z_mean2[:], in0=z_sum[:, 0:1], scalar=1.0 / ROWS**2, in1=z_sum[:, 0:1],
+                op0=ALU.mult, op1=ALU.mult,
             )
             z_padded = small.tile([P, 1], F32)
             nc.vector.tensor_scalar(
-                out=z_padded[:], in0=z_sum[:, 1:2], scalar1=1.0 / ROWS,
-                scalar2=z_mean2_less_eps[:], op0=ALU.mult, op1=ALU.subtract,
+                out=z_padded[:], in0=z_sum[:, 1:2], scalar1=1.0 / ROWS, scalar2=z_mean2[:],
+                op0=ALU.mult, op1=ALU.subtract,
             )
             z_factor = small.tile([P, 1], F32)
             nc.gpsimd.tensor_tensor(
-                out=z_factor[:], in0=z_padded[:], in1=minus_half[:, 0:1], op=ALU.pow
+                out=z_factor[:], in0=z_padded[:], in1=minus_half[:], op=ALU.pow
             )
-            zx_shift = small.tile([P, 1], F32)
+            recentre = small.tile([P, 1], F32)
             nc.vector.tensor_scalar(
-                out=zx_shift[:], in0=z_sum[:, 0:1], scalar1=-1.0 / ROWS, scalar2=z_factor[:],
-                op0=ALU.mult, op1=ALU.mult,
+                out=recentre[:], in0=z_sum[:, 0:1], scalar1=-1.0 / ROWS,
+                scalar2=shift[:, M : M + 1], op0=ALU.mult, op1=ALU.add,
             )
+            store_z(last)
 
-            for j in range(NBLOCKS):
-                zx_t = tail.tile([P, BLOCK], F32)
-                nc.vector.tensor_scalar(
-                    out=zx_t[:], in0=z_less_shift[:, block_cols(j)], scalar1=z_factor[:],
-                    scalar2=zx_shift[:], op0=ALU.mult, op1=ALU.add,
-                )
-                back = transpose_back(zx_t[:])
-                zx_rows = staging.tile([P, SUB * D], F32)
-                nc.scalar.copy(out=zx_rows[:], in_=back[:].rearrange("r s d -> r (s d)"))
-                nc.sync.dma_start(out=block_rows(out_1, j), in_=zx_rows[:])
+            back_of = {}
+            for j in range(NBLOCKS + 2):
+                if j < NBLOCKS:
+                    zx_t = tail.tile([P, BLOCK], F32)
+                    nc.vector.tensor_scalar(
+                        out=zx_t[:], in0=z_less_shift[:, block_cols(j)], scalar1=recentre[:],
+                        scalar2=z_factor[:], op0=ALU.add, op1=ALU.mult,
+                    )
+                    back_of[j] = transpose_back(zx_t[:])
+                if j >= 2:
+                    zx_rows = staging.tile([P, SUB * D], F32)
+                    copy = nc.vector.tensor_copy if j % 4 == 1 else nc.scalar.copy
+                    copy(out=zx_rows[:], in_=back_of[j - 2][:].rearrange("r s d -> r (s d)"))
+                    nc.sync.dma_start(out=block_rows(out_1, j - 2), in_=zx_rows[:])

@@ -61,8 +61,13 @@ def tile_modelvd_pa_t_kernel(tc, en1, W2, b2, Wmean, Wlogvar, eps, out_0, out_1)
         make_identity(nc, ident_f32[:])
         ident_bf16 = keep.tile([P, P], BF16)
         make_identity(nc, ident_bf16[:])
+        z_sums = keep.tile([P, 2, NBLOCKS + 1], F32)
         minus_half = keep.tile([P, 1], F32)
         nc.gpsimd.memset(minus_half[:], -0.5)
+        nc.vector.tensor_scalar(
+            out=z_sums[:, 1, NBLOCKS:], in0=minus_half[:], scalar1=0.0, scalar2=ROWS * BN_EPS,
+            op0=ALU.mult, op1=ALU.add,
+        )
 
         warm = keep.tile([P, 1], F32)
         nc.vector.memset(warm[:], 0.0)
@@ -79,11 +84,11 @@ def tile_modelvd_pa_t_kernel(tc, en1, W2, b2, Wmean, Wlogvar, eps, out_0, out_1)
         eps_t = keep.tile([P, ROWS], BF16)
         stats = keep.tile([P, 2, NBLOCKS, BN_STATS_DIM], F32)
         mean_var = keep.tile([P, 2, 2], F32)
+        minus_mean = keep.tile([P, 2], F32)
         padded = keep.tile([P, 2], F32)
         factor = keep.tile([P, 2], F32)
         shift = keep.tile([P, 2], F32)
         shift_row = keep.tile([P, D], F32)
-        z_sums = keep.tile([P, 2, NBLOCKS + 1], F32)
 
         def head_product(i, j):
             product = psum.tile([P, BLOCK], F32, tag="bank")
@@ -97,6 +102,23 @@ def tile_modelvd_pa_t_kernel(tc, en1, W2, b2, Wmean, Wlogvar, eps, out_0, out_1)
                 stop=True,
             )
             return product
+
+        def transpose_eps(first_block, blocks, copy=nc.scalar.copy):
+            for j in range(first_block, first_block + blocks, 2):
+                eps_ps = psum.tile([P, 2 * SUB, P], BF16, name="eps_ps", tag="bank")
+                for c in range(2 * SUB):
+                    nc.tensor.transpose(
+                        eps_ps[:, c, :], eps_rows[:, j * SUB + c, :], ident_bf16[:]
+                    )
+                if copy is not None:
+                    empty_eps(eps_ps, j, copy)
+            return eps_ps
+
+        def empty_eps(eps_ps, j, copy):
+            copy(
+                out=eps_t[:, j * BLOCK : (j + 2) * BLOCK],
+                in_=eps_ps[:].rearrange("p c r -> p (c r)"),
+            )
 
         with ExitStack() as phase:
             prep = phase.enter_context(tc.tile_pool(name="prep", bufs=1))
@@ -213,18 +235,6 @@ def tile_modelvd_pa_t_kernel(tc, en1, W2, b2, Wmean, Wlogvar, eps, out_0, out_1)
             def take_statistics(i, j):
                 nc.vector.bn_stats(out=stats[:, i, j, :], in_=products_of[j][i][:])
 
-            def transpose_eps(first_block, blocks):
-                for j in range(first_block, first_block + blocks, 2):
-                    eps_ps = psum.tile([P, 2 * SUB, P], BF16, tag="bank")
-                    for c in range(2 * SUB):
-                        nc.tensor.transpose(
-                            eps_ps[:, c, :], eps_rows[:, j * SUB + c, :], ident_bf16[:]
-                        )
-                    nc.scalar.copy(
-                        out=eps_t[:, j * BLOCK : (j + 2) * BLOCK],
-                        in_=eps_ps[:].rearrange("p c r -> p (c r)"),
-                    )
-
             def prepare_w2():
                 w2_grouped = prep.tile([P, PASSES1, K2, PACK], BF16, align_bytes=64)
 
@@ -309,13 +319,15 @@ def tile_modelvd_pa_t_kernel(tc, en1, W2, b2, Wmean, Wlogvar, eps, out_0, out_1)
                 take_statistics(head, last - 2)
             regroup_en2(last - 1)
             first_product(last, pieces=2)
-            transpose_eps(0, 4)
             quantise_en2(last - 1)
             regroup_en2(last, engines=(nc.vector.tensor_copy, nc.scalar.copy))
+            transpose_eps(0, 6)
             products_of[last - 1] = {head: head_product(head, last - 1) for head in (LV, M)}
             quantise_en2(last, pieces=2)
             products_of[last] = {head: head_product(head, last) for head in (LV, M)}
-            transpose_eps(4, NBLOCKS - 4)
+            lv_of = {j: head_product(LV, j) for j in range(2)}
+            transpose_eps(6, 4)
+            eps_last = {j: transpose_eps(j, 2, copy=None) for j in range(10, NBLOCKS, 2)}
 
         with ExitStack() as phase:
             small = phase.enter_context(tc.tile_pool(name="small", bufs=1))
@@ -330,15 +342,17 @@ def tile_modelvd_pa_t_kernel(tc, en1, W2, b2, Wmean, Wlogvar, eps, out_0, out_1)
                     out=padded[:, i : i + 1], in0=mean_var[:, i, 1:2], scalar1=BN_EPS,
                     scalar2=4.0 if i == LV else 1.0, op0=ALU.add, op1=ALU.mult,
                 )
+                nc.vector.tensor_scalar(
+                    out=minus_mean[:, i : i + 1], in0=mean_var[:, i, 0:1], scalar1=-1.0,
+                    scalar2=None, op0=ALU.mult,
+                )
                 nc.gpsimd.tensor_tensor(
                     out=factor[:, i : i + 1], in0=padded[:, i : i + 1], in1=minus_half[:],
                     op=ALU.pow,
                 )
-
-            def make_shift(i):
-                nc.vector.scalar_tensor_tensor(
-                    out=shift[:, i : i + 1], in0=mean_var[:, i, 0:1], scalar=-1.0,
-                    in1=factor[:, i : i + 1], op0=ALU.mult, op1=ALU.mult,
+                nc.gpsimd.tensor_tensor(
+                    out=shift[:, i : i + 1], in0=minus_mean[:, i : i + 1],
+                    in1=factor[:, i : i + 1], op=ALU.mult,
                 )
 
             for j in (last - 1, last):
@@ -347,28 +361,22 @@ def tile_modelvd_pa_t_kernel(tc, en1, W2, b2, Wmean, Wlogvar, eps, out_0, out_1)
             for j in (last - 1, last):
                 take_statistics(M, j)
             finish_statistics(M)
-            make_shift(LV)
-            make_shift(M)
-            nc.vector.tensor_scalar(
-                out=z_sums[:, 0, NBLOCKS:], in0=shift[:, M : M + 1], scalar1=float(ROWS),
-                scalar2=None, op0=ALU.mult,
-            )
-            nc.vector.tensor_scalar(
-                out=z_sums[:, 1, NBLOCKS:], in0=minus_half[:], scalar1=0.0,
-                scalar2=ROWS * BN_EPS, op0=ALU.mult, op1=ALU.add,
-            )
-
-            lv_of = {0: head_product(LV, 0)}
             m_of = {}
+            back_of = {}
             std_of = {}
             noise_of = {}
 
-            shift_ps = psum.tile([P, D], F32, tag="bank")
-            nc.tensor.matmul(
-                out=shift_ps[:], lhsT=shift[:, M : M + 1].to_broadcast([P, P]), rhs=ident_f32[:],
-                start=True, stop=True,
-            )
-            nc.vector.tensor_copy(out=shift_row[:], in_=shift_ps[:])
+            def spread_shift():
+                shift_ps = psum.tile([P, D], F32, tag="bank")
+                nc.tensor.matmul(
+                    out=shift_ps[:], lhsT=shift[:, M : M + 1].to_broadcast([P, P]),
+                    rhs=ident_f32[:], start=True, stop=True,
+                )
+                nc.vector.tensor_copy(out=shift_row[:], in_=shift_ps[:])
+                nc.scalar.activation(
+                    out=z_sums[:, 0, NBLOCKS:], in_=shift[:, M : M + 1], func=ACT.Copy,
+                    scale=float(ROWS),
+                )
 
             z_less_shift = small.tile([P, ROWS], F32)
 
@@ -382,7 +390,8 @@ def tile_modelvd_pa_t_kernel(tc, en1, W2, b2, Wmean, Wlogvar, eps, out_0, out_1)
 
             def noise_block(j):
                 noise = tail.tile([P, BLOCK], F32)
-                nc.gpsimd.tensor_tensor(
+                engine = nc.vector if j == 0 else nc.gpsimd
+                engine.tensor_tensor(
                     out=noise[:], in0=std_of[j][:], in1=eps_t[:, block_cols(j)], op=ALU.mult
                 )
                 noise_of[j] = noise
@@ -408,10 +417,9 @@ def tile_modelvd_pa_t_kernel(tc, en1, W2, b2, Wmean, Wlogvar, eps, out_0, out_1)
                 return back
 
             def store_z(j):
-                back = transpose_back(z_less_shift[:, block_cols(j)])
                 z_rows = staging.tile([P, SUB, D], F32)
                 nc.vector.tensor_tensor(
-                    out=z_rows[:], in0=back[:],
+                    out=z_rows[:], in0=back_of[j][:],
                     in1=shift_row[:].unsqueeze(1).to_broadcast([P, SUB, D]), op=ALU.add,
                 )
                 nc.sync.dma_start(
@@ -419,21 +427,34 @@ def tile_modelvd_pa_t_kernel(tc, en1, W2, b2, Wmean, Wlogvar, eps, out_0, out_1)
                 )
 
             for j in range(NBLOCKS + 2):
-                if j + 1 < NBLOCKS:
-                    lv_of[j + 1] = head_product(LV, j + 1)
-                if 1 <= j <= NBLOCKS:
-                    m_of[j - 1] = head_product(M, j - 1)
+                if j % 2 == 0:
+                    for k in (j + 2, j + 3):
+                        if k < NBLOCKS:
+                            lv_of[k] = head_product(LV, k)
+                    for k in (j - 1, j):
+                        if 0 <= k < NBLOCKS:
+                            m_of[k] = head_product(M, k)
+                    for k in (j - 4, j - 3):
+                        if 0 <= k:
+                            back_of[k] = transpose_back(z_less_shift[:, block_cols(k)])
                 if j < NBLOCKS:
                     std_block(j)
                 if 1 <= j <= NBLOCKS:
                     noise_block(j - 1)
+                if j < 2:
+                    for k in (10,) if j == 0 else (12, 14):
+                        empty_eps(eps_last[k], k, nc.vector.tensor_copy)
                 if 2 <= j:
                     sample_block(j - 2)
+                if j == 3:
+                    spread_shift()
                 if j >= 3:
                     square_block(j - 3)
                 if j >= 4:
                     store_z(j - 4)
             square_block(last)
+            for k in (last - 1, last):
+                back_of[k] = transpose_back(z_less_shift[:, block_cols(k)])
             store_z(last - 1)
 
             z_sum = small.tile([P, 2], F32)
@@ -457,9 +478,7 @@ def tile_modelvd_pa_t_kernel(tc, en1, W2, b2, Wmean, Wlogvar, eps, out_0, out_1)
                 out=recentre[:], in0=z_sum[:, 0:1], scalar1=-1.0 / ROWS,
                 scalar2=shift[:, M : M + 1], op0=ALU.mult, op1=ALU.add,
             )
-            store_z(last)
-
-            back_of = {}
+            zx_back_of = {}
             for j in range(NBLOCKS + 2):
                 if j < NBLOCKS:
                     zx_t = tail.tile([P, BLOCK], F32)
@@ -467,9 +486,11 @@ def tile_modelvd_pa_t_kernel(tc, en1, W2, b2, Wmean, Wlogvar, eps, out_0, out_1)
                         out=zx_t[:], in0=z_less_shift[:, block_cols(j)], scalar1=recentre[:],
                         scalar2=z_factor[:], op0=ALU.add, op1=ALU.mult,
                     )
-                    back_of[j] = transpose_back(zx_t[:])
+                    zx_back_of[j] = transpose_back(zx_t[:])
+                if j == 1:
+                    store_z(last)
                 if j >= 2:
                     zx_rows = staging.tile([P, SUB * D], F32)
                     copy = nc.vector.tensor_copy if j % 4 == 1 else nc.scalar.copy
-                    copy(out=zx_rows[:], in_=back_of[j - 2][:].rearrange("r s d -> r (s d)"))
+                    copy(out=zx_rows[:], in_=zx_back_of[j - 2][:].rearrange("r s d -> r (s d)"))
                     nc.sync.dma_start(out=block_rows(out_1, j - 2), in_=zx_rows[:])

@@ -188,11 +188,13 @@ def tile_modelvd_pa_t_kernel(tc, en1, W2, b2, Wmean, Wlogvar, eps, out_0, out_1)
                     )
                 en1_mx_of[j] = (codes, scales)
 
-            def first_product(j, pieces=1):
+            def first_product(j, pieces=1, chosen=(0, 1)):
                 codes, scales = en1_mx_of[j]
-                planes = work.tile([P, K2_TILES, BLOCK], BF16)
+                if j not in planes_of:
+                    planes_of[j] = work.tile([P, K2_TILES, BLOCK], BF16, name="planes")
+                planes = planes_of[j]
                 width = BLOCK // pieces
-                for c in range(pieces):
+                for c in chosen[0:pieces]:
                     for t in range(K2_TILES):
                         h = psum.tile([P, width], F32, tag="bank")
                         for g in range(PASSES1):
@@ -210,7 +212,6 @@ def tile_modelvd_pa_t_kernel(tc, en1, W2, b2, Wmean, Wlogvar, eps, out_0, out_1)
                             out=planes[:, t, c * width : (c + 1) * width], in_=h[:],
                             func=ACT.Relu, bias=bias[:, t : t + 1],
                         )
-                planes_of[j] = planes
 
             def regroup_en2(j, engines=(nc.vector.tensor_copy,)):
                 grouped2 = work.tile([P, BLOCK, PACK], BF16, align_bytes=64)
@@ -288,9 +289,11 @@ def tile_modelvd_pa_t_kernel(tc, en1, W2, b2, Wmean, Wlogvar, eps, out_0, out_1)
             transpose_block(0)
             quantise_en1(0, pieces=2)
             nc.gpsimd.tensor_copy(out=bias[:], in_=b2_cols[:])
-            first_product(0, pieces=2)
+            first_product(0, pieces=2, chosen=(0,))
             transpose_block(1)
+            first_product(0, pieces=2, chosen=(1,))
             prepare_heads()
+            sort_words(2)
             quantise_en1(1)
             load_block(LOADS_AHEAD)
 

from contextlib import ExitStack

import concourse.mybir as mybir
from concourse.masks import make_identity

F32 = mybir.dt.float32
BF16 = mybir.dt.bfloat16
U32 = mybir.dt.uint32
U8 = mybir.dt.uint8
FP8X4 = mybir.dt.float8_e4m3fn_x4
ACT = mybir.ActivationFunctionType
ALU = mybir.AluOpType
AXIS = mybir.AxisListType

P = 128
PACK = 4
ROWS = 8192
K1 = 1024
K2 = 512
D = 128
PASSES1 = K1 // (P * PACK)
BLOCK = 512
NBLOCKS = ROWS // BLOCK
SUB = BLOCK // P
K2_TILES = K2 // P
PSUM_BANKS = 8
BN_EPS = 1e-5
BN_STATS_DIM = 6
LOADS_AHEAD = 3
M = 0
LV = 1
HALF = BLOCK // 2
SORTED = 2

FLOPS = 2 * ROWS * (K1 * K2 + K2 * 2 * D)


def block_cols(j):
    return slice(j * BLOCK, (j + 1) * BLOCK)


def block_rows(dram, j):
    return dram[j * BLOCK : (j + 1) * BLOCK, :].rearrange("(r s) w -> r (s w)", s=SUB)


def regrouped(grouped, planes):
    return {
        "out": grouped.rearrange("p (c i) t -> p c t i", i=4),
        "in_": planes.rearrange("p t (c i) -> p c t i", i=4),
    }


def tile_modelvd_pa_t_kernel(tc, en1, W2, b2, Wmean, Wlogvar, eps, out_0, out_1):
    nc = tc.nc
    with ExitStack() as kernel_scope:
        kernel_scope.enter_context(tc.manual_schedule())
        keep = kernel_scope.enter_context(tc.tile_pool(name="keep", bufs=1))
        psum = kernel_scope.enter_context(tc.psum_pool(name="psum", bufs=PSUM_BANKS))

        ident_f32 = keep.tile([P, P], F32)
        make_identity(nc, ident_f32[:])
        ident_bf16 = keep.tile([P, P], BF16)
        make_identity(nc, ident_bf16[:])
        z_sums = keep.tile([P, 2, NBLOCKS + 1], F32)
        minus_half = keep.tile([P, 1], F32)
        nc.gpsimd.memset(minus_half[:], -0.5)
        nc.vector.tensor_scalar(
            out=z_sums[:, 1, NBLOCKS:], in0=minus_half[:], scalar1=0.0, scalar2=ROWS * BN_EPS,
            op0=ALU.mult, op1=ALU.add,
        )

        warm = keep.tile([P, 1], F32)
        nc.vector.memset(warm[:], 0.0)
        nc.scalar.activation(out=warm[:], in_=warm[:], func=ACT.Exp)

        w2_codes = keep.tile([P, PASSES1, K2], U32, align_bytes=64)
        w2_scales = keep.tile([P, PASSES1, K2], U8, align_bytes=64)
        head_codes = keep.tile([P, 2, D], U32, align_bytes=64)
        head_scales = keep.tile([P, 2, D], U8, align_bytes=64)
        bias = keep.tile([P, K2_TILES], F32)
        en2_codes = keep.tile([P, ROWS], U32, align_bytes=64)
        en2_scales = keep.tile([P, ROWS], U8, align_bytes=64)
        eps_rows = keep.tile([P, NBLOCKS * SUB, D], BF16)
        eps_t = keep.tile([P, ROWS], BF16)
        stats = keep.tile([P, 2, NBLOCKS, BN_STATS_DIM], F32)
        mean_var = keep.tile([P, 2, 2], F32)
        minus_mean = keep.tile([P, 2], F32)
        padded = keep.tile([P, 2], F32)
        factor = keep.tile([P, 2], F32)
        shift = keep.tile([P, 2], F32)
        shift_row = keep.tile([P, D], F32)

        def head_product(i, j):
            product = psum.tile([P, BLOCK], F32, tag="bank")
            nc.tensor.matmul_mx(
                out=product[:],
                lhsT=head_codes[:, i, :].bitcast(FP8X4),
                lhsT_scale=head_scales[:, i, :],
                rhs=en2_codes[:, block_cols(j)].bitcast(FP8X4),
                rhs_scale=en2_scales[:, block_cols(j)],
                start=True,
                stop=True,
            )
            return product

        def transpose_eps(first_block, blocks, copy=nc.scalar.copy):
            for j in range(first_block, first_block + blocks, 2):
                eps_ps = psum.tile([P, 2 * SUB, P], BF16, name="eps_ps", tag="bank")
                for c in range(2 * SUB):
                    nc.tensor.transpose(
                        eps_ps[:, c, :], eps_rows[:, j * SUB + c, :], ident_bf16[:]
                    )
                if copy is not None:
                    empty_eps(eps_ps, j, copy)
            return eps_ps

        def empty_eps(eps_ps, j, copy):
            copy(
                out=eps_t[:, j * BLOCK : (j + 2) * BLOCK],
                in_=eps_ps[:].rearrange("p c r -> p (c r)"),
            )

        with ExitStack() as phase:
            prep = phase.enter_context(tc.tile_pool(name="prep", bufs=1))
            loads = phase.enter_context(tc.tile_pool(name="loads", bufs=LOADS_AHEAD + 1))
            work = phase.enter_context(tc.tile_pool(name="work", bufs=2))

            x_of = {}
            sorted_of = {}
            grouped1_of = {}
            en1_mx_of = {}
            planes_of = {}
            grouped2_of = {}
            products_of = {}

            def load_block(j, pieces=1):
                x = loads.tile([P, SUB * K1], BF16, name="x")
                width = SUB * K1 // pieces
                for c in range(pieces):
                    cols = slice(c * width, (c + 1) * width)
                    nc.sync.dma_start(out=x[:, cols], in_=block_rows(en1, j)[:, cols])
                x_of[j] = x

            def sort_words(j):
                words = x_of[j][:].bitcast(F32).rearrange("p (s w u) -> p s u w", s=SUB, u=2)
                in_order = work.tile([P, SORTED, 2, K1 // 4], F32)
                nc.vector.tensor_copy(out=in_order[:], in_=words[:, 0:SORTED])
                sorted_of[j] = in_order

            def transpose_block(j):
                words = x_of[j][:].bitcast(F32).rearrange("p (s w) -> p s w", s=SUB)
                grouped1 = work.tile([P, PASSES1 * BLOCK * PACK], BF16, align_bytes=64)
                pairs = grouped1[:].bitcast(F32).rearrange(
                    "p (g h s r u) -> p g h s r u", g=PASSES1, h=2, s=2, r=P, u=2
                )
                for half in range(2):
                    for g in range(PASSES1):
                        xt = psum.tile([P, 2, 2, P], F32, tag="bank")
                        for s in range(2):
                            piece = 2 * half + s
                            for u in range(2):
                                if j in sorted_of and piece < SORTED:
                                    taken = sorted_of[j][:, piece, u, g * P : (g + 1) * P]
                                else:
                                    taken = words[:, piece, 2 * g * P + u : 2 * (g + 1) * P : 2]
                                nc.tensor.transpose(xt[:, s, u, :], taken, ident_f32[:])
                        nc.scalar.copy(
                            out=pairs[:, g, half], in_=xt[:].rearrange("p s u r -> p s r u")
                        )
                grouped1_of[j] = grouped1

            def quantise_en1(j, pieces=1):
                codes = work.tile([P, PASSES1 * BLOCK], U32, name="en1_codes", align_bytes=64)
                scales = work.tile([P, PASSES1 * BLOCK], U8, name="en1_scales", align_bytes=64)
                if pieces == 1:
                    runs = [slice(0, PASSES1 * BLOCK)]
                else:
                    runs = [
                        slice(g * BLOCK + half * HALF, g * BLOCK + (half + 1) * HALF)
                        for half in range(2)
                        for g in range(PASSES1)
                    ]
                for run in runs:
                    nc.vector.quantize_mx(
                        out=codes[:, run].bitcast(FP8X4),
                        scales=scales[:, run],
                        in_=grouped1_of[j][:, run.start * PACK : run.stop * PACK],
                    )
                en1_mx_of[j] = (codes, scales)

            def first_product(j, pieces=1, chosen=(0, 1)):
                codes, scales = en1_mx_of[j]
                if j not in planes_of:
                    planes_of[j] = work.tile([P, K2_TILES, BLOCK], BF16, name="planes")
                planes = planes_of[j]
                width = BLOCK // pieces
                for c in chosen[0:pieces]:
                    for t in range(K2_TILES):
                        h = psum.tile([P, width], F32, tag="bank")
                        for g in range(PASSES1):
                            run = slice(g * BLOCK + c * width, g * BLOCK + (c + 1) * width)
                            nc.tensor.matmul_mx(
                                out=h[:],
                                lhsT=w2_codes[:, g, t * P : (t + 1) * P].bitcast(FP8X4),
                                lhsT_scale=w2_scales[:, g, t * P : (t + 1) * P],
                                rhs=codes[:, run].bitcast(FP8X4),
                                rhs_scale=scales[:, run],
                                start=(g == 0),
                                stop=(g == PASSES1 - 1),
                            )
                        nc.scalar.activation(
                            out=planes[:, t, c * width : (c + 1) * width], in_=h[:],
                            func=ACT.Relu, bias=bias[:, t : t + 1],
                        )

            def regroup_en2(j, engines=(nc.vector.tensor_copy,)):
                grouped2 = work.tile([P, BLOCK, PACK], BF16, align_bytes=64)
                width = BLOCK // len(engines)
                for c, copy in enumerate(engines):
                    cols = slice(c * width, (c + 1) * width)
                    copy(**regrouped(grouped2[:, cols], planes_of[j][:, :, cols]))
                grouped2_of[j] = grouped2

            def quantise_en2(j, pieces=1):
                width = BLOCK // pieces
                for c in range(pieces):
                    cols = slice(j * BLOCK + c * width, j * BLOCK + (c + 1) * width)
                    nc.vector.quantize_mx(
                        out=en2_codes[:, cols].bitcast(FP8X4),
                        scales=en2_scales[:, cols],
                        in_=grouped2_of[j][:, c * width : (c + 1) * width].rearrange(
                            "p c t -> p (c t)"
                        ),
                    )

            def take_statistics(i, j):
                nc.vector.bn_stats(out=stats[:, i, j, :], in_=products_of[j][i][:])

            def prepare_w2():
                w2_grouped = prep.tile([P, PASSES1, K2, PACK], BF16, align_bytes=64)

                def regroup_w2(copy, g, first_tile, last_tile):
                    tiles = slice(first_tile, last_tile)
                    copy(
                        out=w2_grouped[:, g].rearrange("p (t m) j -> p t m j", t=K2_TILES)[:, tiles],
                        in_=w2_rows[:, g].rearrange("p j (m t) -> p t m j", t=K2_TILES)[:, tiles],
                    )

                regroup_w2(nc.vector.tensor_copy, 0, 0, K2_TILES)
                regroup_w2(nc.scalar.copy, 1, K2_TILES // 2, K2_TILES)
                regroup_w2(nc.vector.tensor_copy, 1, 0, K2_TILES // 2)
                for g in range(PASSES1):
                    nc.vector.quantize_mx(
                        out=w2_codes[:, g, :].bitcast(FP8X4),
                        scales=w2_scales[:, g, :],
                        in_=w2_grouped[:, g].rearrange("p c t -> p (c t)"),
                    )

            def prepare_heads():
                head_grouped = prep.tile([P, 2, D, PACK], BF16, align_bytes=64)
                for i in (M, LV):
                    nc.vector.tensor_copy(**regrouped(head_grouped[:, i], head_rows[:, i]))
                nc.vector.quantize_mx(
                    out=head_codes[:].rearrange("p i d -> p (i d)").bitcast(FP8X4),
                    scales=head_scales[:].rearrange("p i d -> p (i d)"),
                    in_=head_grouped[:].rearrange("p i d t -> p (i d t)"),
                )

            w2_rows = prep.tile([P, PASSES1, PACK, K2], BF16)
            for g in range(PASSES1):
                nc.sync.dma_start(
                    out=w2_rows[:, g].rearrange("p j c -> p (j c)"),
                    in_=W2[g * P * PACK : (g + 1) * P * PACK, :].rearrange(
                        "(p j) c -> p (j c)", j=PACK
                    ),
                )
            load_block(0, pieces=2)
            b2_cols = prep.tile([P, K2_TILES], BF16)
            nc.sync.dma_start(out=b2_cols[:], in_=b2.rearrange("(p t) -> p t", t=K2_TILES))
            load_block(1)
            head_rows = prep.tile([P, 2, PACK, D], BF16)
            for i, weight in ((M, Wmean), (LV, Wlogvar)):
                nc.sync.dma_start(
                    out=head_rows[:, i], in_=weight.rearrange("(p t) d -> p t d", t=PACK)
                )
            load_block(2)

            prepare_w2()
            transpose_block(0)
            quantise_en1(0, pieces=2)
            nc.gpsimd.tensor_copy(out=bias[:], in_=b2_cols[:])
            first_product(0, pieces=2, chosen=(0,))
            transpose_block(1)
            first_product(0, pieces=2, chosen=(1,))
            prepare_heads()
            sort_words(2)
            quantise_en1(1)
            load_block(LOADS_AHEAD)

            for i in range(1, NBLOCKS - 1):
                if i + LOADS_AHEAD < NBLOCKS:
                    load_block(i + LOADS_AHEAD)
                if i + LOADS_AHEAD == NBLOCKS:
                    nc.sync.dma_start(
                        out=eps_rows[:].rearrange("r (j s) d -> r j (s d)", s=SUB),
                        in_=eps.rearrange("(j r s) d -> r j (s d)", r=P, s=SUB),
                    )
                if i >= 2:
                    for head in (M, LV):
                        take_statistics(head, i - 2)
                regroup_en2(i - 1)
                if i + 2 < NBLOCKS:
                    sort_words(i + 2)
                transpose_block(i + 1)
                quantise_en2(i - 1)
                quantise_en1(i + 1)
                first_product(i)
                products_of[i - 1] = {head: head_product(head, i - 1) for head in (M, LV)}

            last = NBLOCKS - 1
            for head in (M, LV):
                take_statistics(head, last - 2)
            regroup_en2(last - 1)
            first_product(last, pieces=2)
            quantise_en2(last - 1)
            regroup_en2(last, engines=(nc.vector.tensor_copy, nc.scalar.copy))
            transpose_eps(0, 6)
            products_of[last - 1] = {head: head_product(head, last - 1) for head in (LV, M)}
            quantise_en2(last, pieces=2)
            products_of[last] = {head: head_product(head, last) for head in (LV, M)}
            lv_of = {j: head_product(LV, j) for j in range(2)}
            transpose_eps(6, 4)
            eps_last = {j: transpose_eps(j, 2, copy=None) for j in range(10, NBLOCKS, 2)}

        with ExitStack() as phase:
            small = phase.enter_context(tc.tile_pool(name="small", bufs=1))
            tail = phase.enter_context(tc.tile_pool(name="tail", bufs=4))
            staging = phase.enter_context(tc.tile_pool(name="staging", bufs=6))

            def finish_statistics(i):
                nc.vector.bn_aggr(
                    out=mean_var[:, i, :], in_=stats[:, i].rearrange("p j v -> p (j v)")
                )
                nc.vector.tensor_scalar(
                    out=padded[:, i : i + 1], in0=mean_var[:, i, 1:2], scalar1=BN_EPS,
                    scalar2=4.0 if i == LV else 1.0, op0=ALU.add, op1=ALU.mult,
                )
                nc.vector.tensor_scalar(
                    out=minus_mean[:, i : i + 1], in0=mean_var[:, i, 0:1], scalar1=-1.0,
                    scalar2=None, op0=ALU.mult,
                )
                nc.gpsimd.tensor_tensor(
                    out=factor[:, i : i + 1], in0=padded[:, i : i + 1], in1=minus_half[:],
                    op=ALU.pow,
                )
                nc.gpsimd.tensor_tensor(
                    out=shift[:, i : i + 1], in0=minus_mean[:, i : i + 1],
                    in1=factor[:, i : i + 1], op=ALU.mult,
                )

            for j in (last - 1, last):
                take_statistics(LV, j)
            finish_statistics(LV)
            for j in (last - 1, last):
                take_statistics(M, j)
            finish_statistics(M)
            m_of = {}
            back_of = {}
            std_of = {}
            noise_of = {}

            def spread_shift():
                shift_ps = psum.tile([P, D], F32, tag="bank")
                nc.tensor.matmul(
                    out=shift_ps[:], lhsT=shift[:, M : M + 1].to_broadcast([P, P]),
                    rhs=ident_f32[:], start=True, stop=True,
                )
                nc.vector.tensor_copy(out=shift_row[:], in_=shift_ps[:])
                nc.scalar.activation(
                    out=z_sums[:, 0, NBLOCKS:], in_=shift[:, M : M + 1], func=ACT.Copy,
                    scale=float(ROWS),
                )

            z_less_shift = small.tile([P, ROWS], F32)

            def std_block(j):
                std = tail.tile([P, BLOCK], F32)
                nc.scalar.activation(
                    out=std[:], in_=lv_of[j][:], func=ACT.Exp,
                    bias=shift[:, LV : LV + 1], scale=factor[:, LV : LV + 1],
                )
                std_of[j] = std

            def noise_block(j):
                noise = tail.tile([P, BLOCK], F32)
                engine = nc.vector if j == 0 else nc.gpsimd
                engine.tensor_tensor(
                    out=noise[:], in0=std_of[j][:], in1=eps_t[:, block_cols(j)], op=ALU.mult
                )
                noise_of[j] = noise

            def sample_block(j):
                nc.vector.scalar_tensor_tensor(
                    out=z_less_shift[:, block_cols(j)], in0=m_of[j][:],
                    scalar=factor[:, M : M + 1], in1=noise_of[j][:],
                    op0=ALU.mult, op1=ALU.add, accum_out=z_sums[:, 0, j : j + 1],
                )

            def square_block(j):
                squares = tail.tile([P, BLOCK], F32)
                nc.scalar.activation(
                    out=squares[:], in_=z_less_shift[:, block_cols(j)], func=ACT.Square,
                    bias=shift[:, M : M + 1], accum_out=z_sums[:, 1, j : j + 1],
                )

            def transpose_back(source):
                back = psum.tile([P, SUB, D], F32, tag="bank")
                for s in range(SUB):
                    nc.tensor.transpose(back[:, s, :], source[:, s * P : (s + 1) * P], ident_f32[:])
                return back

            def store_z(j):
                z_rows = staging.tile([P, SUB, D], F32)
                nc.vector.tensor_tensor(
                    out=z_rows[:], in0=back_of[j][:],
                    in1=shift_row[:].unsqueeze(1).to_broadcast([P, SUB, D]), op=ALU.add,
                )
                nc.sync.dma_start(
                    out=block_rows(out_0, j), in_=z_rows[:].rearrange("r s d -> r (s d)")
                )

            for j in range(NBLOCKS + 2):
                if j % 2 == 0:
                    for k in (j + 2, j + 3):
                        if k < NBLOCKS:
                            lv_of[k] = head_product(LV, k)
                    for k in (j - 1, j):
                        if 0 <= k < NBLOCKS:
                            m_of[k] = head_product(M, k)
                    for k in (j - 4, j - 3):
                        if 0 <= k:
                            back_of[k] = transpose_back(z_less_shift[:, block_cols(k)])
                if j < NBLOCKS:
                    std_block(j)
                if 1 <= j <= NBLOCKS:
                    noise_block(j - 1)
                if j < 2:
                    for k in (10,) if j == 0 else (12, 14):
                        empty_eps(eps_last[k], k, nc.vector.tensor_copy)
                if 2 <= j:
                    sample_block(j - 2)
                if j == 3:
                    spread_shift()
                if j >= 3:
                    square_block(j - 3)
                if j >= 4:
                    store_z(j - 4)
            square_block(last)
            for k in (last - 1, last):
                back_of[k] = transpose_back(z_less_shift[:, block_cols(k)])
            store_z(last - 1)

            z_sum = small.tile([P, 2], F32)
            nc.vector.tensor_reduce(out=z_sum[:], in_=z_sums[:], axis=AXIS.X, op=ALU.add)
            z_mean2 = small.tile([P, 1], F32)
            nc.vector.scalar_tensor_tensor(
                out=z_mean2[:], in0=z_sum[:, 0:1], scalar=1.0 / ROWS**2, in1=z_sum[:, 0:1],
                op0=ALU.mult, op1=ALU.mult,
            )
            z_padded = small.tile([P, 1], F32)
            nc.vector.tensor_scalar(
                out=z_padded[:], in0=z_sum[:, 1:2], scalar1=1.0 / ROWS, scalar2=z_mean2[:],
                op0=ALU.mult, op1=ALU.subtract,
            )
            z_factor = small.tile([P, 1], F32)
            nc.gpsimd.tensor_tensor(
                out=z_factor[:], in0=z_padded[:], in1=minus_half[:], op=ALU.pow
            )
            recentre = small.tile([P, 1], F32)
            nc.vector.tensor_scalar(
                out=recentre[:], in0=z_sum[:, 0:1], scalar1=-1.0 / ROWS,
                scalar2=shift[:, M : M + 1], op0=ALU.mult, op1=ALU.add,
            )
            zx_back_of = {}
            for j in range(NBLOCKS + 2):
                if j < NBLOCKS:
                    zx_t = tail.tile([P, BLOCK], F32)
                    nc.vector.tensor_scalar(
                        out=zx_t[:], in0=z_less_shift[:, block_cols(j)], scalar1=recentre[:],
                        scalar2=z_factor[:], op0=ALU.add, op1=ALU.mult,
                    )
                    zx_back_of[j] = transpose_back(zx_t[:])
                if j == 1:
                    store_z(last)
                if j >= 2:
                    zx_rows = staging.tile([P, SUB * D], F32)
                    copy = nc.vector.tensor_copy if j % 4 == 1 else nc.scalar.copy
                    copy(out=zx_rows[:], in_=zx_back_of[j - 2][:].rearrange("r s d -> r (s d)"))
                    nc.sync.dma_start(out=block_rows(out_1, j - 2), in_=zx_rows[:])
